import numpy as np
import ml_dtypes


def mxq(x, axis, fmt="e4m3"):
    dtype, down = {"e4m3": (ml_dtypes.float8_e4m3fn, 7), "e5m2": (ml_dtypes.float8_e5m2, 14)}[fmt]
    v = np.moveaxis(np.asarray(x, np.float32).astype(ml_dtypes.bfloat16).astype(np.float64), axis, -1)
    blocks = v.reshape(v.shape[:-1] + (-1, 32))
    amax = np.abs(blocks).max(-1, keepdims=True)
    byte = np.maximum(np.where(amax > 0, np.frexp(amax)[1] - 1 + 127, 0) - down, 1)
    scale = np.exp2(byte - 127.0)
    codes = (blocks / scale).astype(np.float32).astype(dtype).astype(np.float64)
    return np.moveaxis((codes * scale).reshape(v.shape), -1, axis)


WIDE = False


def mx_kscale(k):
    if not WIDE:
        return np.ones(k)
    levels = np.array([10, -10, 5, -5, 0])
    a = np.random.permutation(np.resize(levels, k // 512 * 4)).reshape(k // 512, 4)
    idx = np.arange(k)
    return np.exp2(a[idx // 512, idx % 128 // 32])


BF16 = ml_dtypes.bfloat16


def bf(x):
    return np.asarray(x, np.float32).astype(BF16)


def f64(x):
    return np.asarray(x).astype(np.float64)


E2M1 = np.array([0.0, 0.5, 1.0, 1.5, 2.0, 3.0, 4.0, 6.0, -0.0, -0.5, -1.0, -1.5, -2.0, -3.0, -4.0, -6.0])


def pack_weight(w, fmt):
    k, n = w.shape
    w = f64(bf(w)).reshape(k // 32, 32, n)
    amax = np.abs(w).max(1)
    if fmt == "e4m3":
        byte = np.frexp(amax)[1] - 1 + 127 - 7
    else:
        mant, ex = np.frexp(amax / 6.0)
        byte = np.where(mant > 0.5, ex, ex - 1) + 127
    byte = np.clip(np.where(amax > 0, byte, 1), 1, 254)
    scaled = (w * np.exp2(127.0 - byte)[:, None, :]).reshape(k, n).astype(np.float32)
    by_word = np.ascontiguousarray(scaled.reshape(k // 512, 128, 4, n).transpose(0, 1, 3, 2))
    if fmt == "e4m3":
        words = by_word.astype(ml_dtypes.float8_e4m3fn).view(np.uint8)
    else:
        c = by_word.astype(ml_dtypes.float4_e2m1fn).view(np.uint8) & 0xF
        words = c[..., 0::2] | (c[..., 1::2] << 4)
    return np.ascontiguousarray(words), np.ascontiguousarray(byte.astype(np.uint8).reshape(k // 512, 16, n))


def unpack_weight(words, scales, fmt):
    g, p, n, _ = words.shape
    if fmt == "e4m3":
        vals = np.ascontiguousarray(words).view(ml_dtypes.float8_e4m3fn).astype(np.float64)
    else:
        nib = np.empty((g, p, n, 4), np.uint8)
        nib[..., 0::2] = words & 0xF
        nib[..., 1::2] = words >> 4
        vals = E2M1[nib]
    vals = vals * np.repeat(np.exp2(scales.astype(np.float64) - 127.0), 8, axis=1)[..., None]
    return vals.transpose(0, 1, 3, 2).reshape(g * 512, n)

def pack4(w):
    words, scales = pack_weight(w, "e2m1")
    return words.reshape(words.shape[0], 128, -1), scales


def unpack4(words, scales):
    return unpack_weight(words.reshape(words.shape[0], 128, -1, 2), scales, "e2m1")


B, N, NODE_IN, EDGE_IN, EDGE_OUT = 2, 64, 192, 128, 512
D_IN = 2 * NODE_IN + EDGE_IN
HID = 2 * EDGE_OUT
NEG_SLOPE = 0.1


def leaky_relu(v):
    return np.where(v >= 0.0, v, NEG_SLOPE * v)


def setup_inputs():
    s = mx_kscale(D_IN)
    sn, se = s[:NODE_IN], s[2 * NODE_IN:]
    st = np.concatenate([sn, sn, se])
    node_fts = bf(np.random.standard_normal((B, N, NODE_IN)) * sn)
    edge_fts = bf(np.random.standard_normal((B, N * N, EDGE_IN)) * se)
    wt = np.random.standard_normal((HID, D_IN)) / np.sqrt(D_IN) / st
    words, scales = pack4(np.ascontiguousarray(wt.T))
    return {"node_fts": node_fts,
            "edge_fts": edge_fts,
            "Wt_words": words,
            "Wt_scales": scales}


def reference(node_fts, edge_fts, Wt_words, Wt_scales):
    node = f64(node_fts)
    src = np.repeat(node, N, axis=1)
    dst = np.tile(node, (1, N, 1))
    triplet = np.concatenate([src, dst, f64(edge_fts)], axis=-1)
    return leaky_relu(mxq(triplet, 2, "e4m3") @ unpack4(Wt_words, Wt_scales))

@@ -1,0 +1,208 @@
+from contextlib import ExitStack
+
+import concourse.masks as masks
+import concourse.mybir as mybir
+
+F32 = mybir.dt.float32
+BF16 = mybir.dt.bfloat16
+I32 = mybir.dt.int32
+U32 = mybir.dt.uint32
+U8 = mybir.dt.uint8
+FP8X4 = mybir.dt.float8_e4m3fn_x4
+FP4X4 = mybir.dt.float4_e2m1fn_x4
+ALU = mybir.AluOpType
+
+P = 128
+PACK = 4
+GRAPHS = 2
+NODES = 64
+NODE_IN = 192
+EDGE_IN = 128
+HID = 1024
+NEG_SLOPE = 0.1
+BANK = 512
+HALVES = HID // BANK
+
+TILES = NODES
+PAIR = 2
+PAIRS = TILES // PAIR
+
+DST_P = NODE_IN // PACK
+SRC_END = 2 * DST_P
+EDGE_P0 = SRC_END
+
+NODE_W = NODE_IN // 2
+EDGE_W = EDGE_IN // 2
+FRONT_W = 2 * NODE_W
+ROW_W = P * PACK // 2
+LOAD_TILES = 8
+
+FLOPS = 2 * GRAPHS * NODES * NODES * (2 * NODE_IN + EDGE_IN) * HID
+
+
+def tile_edge_update_only_pa_t_kernel(tc, node_fts, edge_fts, Wt_words, Wt_scales, out):
+    nc = tc.nc
+    node_rows = node_fts.rearrange("b n f -> (b n) f")
+    edge_rows = edge_fts.rearrange("b (i k) f -> (b i) (k f)", k=NODES)
+    out_rows = out.rearrange("b (i k) n -> (b i) (k n)", k=NODES)
+
+    with ExitStack() as ctx:
+        ctx.enter_context(tc.manual_schedule())
+        keep = ctx.enter_context(tc.tile_pool(name="keep", bufs=1))
+        quantised = ctx.enter_context(tc.tile_pool(name="quantised", bufs=3))
+        results = ctx.enter_context(tc.tile_pool(name="results", bufs=4))
+        flipped = ctx.enter_context(tc.psum_pool(name="flipped", bufs=2))
+        sums = ctx.enter_context(tc.psum_pool(name="sums", bufs=6))
+
+        rows = keep.tile([P, 2 * (FRONT_W + TILES * EDGE_W)], BF16)
+        nc.sync.dma_start(out=rows[:, 0:NODE_IN], in_=node_rows)
+        nc.sync.dma_start(out=rows[:, NODE_IN : 2 * NODE_IN], in_=node_rows)
+
+        def load_edges(first_tile):
+            first = first_tile * EDGE_IN
+            last = (first_tile + LOAD_TILES) * EDGE_IN
+            nc.sync.dma_start(out=rows[:, 2 * NODE_IN + first : 2 * NODE_IN + last], in_=edge_rows[:, first:last])
+
+        load_edges(0)
+
+        w_codes = keep.tile([P, 2 * HID], U8, align_bytes=64)
+        given_words = Wt_words.bitcast(I32)
+        nc.sync.dma_start(out=w_codes[0:DST_P, :].bitcast(I32), in_=given_words[0, DST_P:SRC_END, :])
+        nc.sync.dma_start(out=w_codes[DST_P:SRC_END, :].bitcast(I32), in_=given_words[0, 0:DST_P, :])
+        nc.sync.dma_start(out=w_codes[EDGE_P0:P, :].bitcast(I32), in_=given_words[0, EDGE_P0:P, :])
+
+        w_scales = keep.tile([P, HID], U8, align_bytes=64)
+        nc.vector.memset(w_scales[:].bitcast(I32), 0)
+        given_scales = Wt_scales.bitcast(I32)
+        nc.sync.dma_start(out=w_scales[0:4, :].bitcast(I32), in_=given_scales[0, 6:10, :])
+        nc.sync.dma_start(out=w_scales[32:34, :].bitcast(I32), in_=given_scales[0, 10:12, :])
+        nc.sync.dma_start(out=w_scales[34:36, :].bitcast(I32), in_=given_scales[0, 0:2, :])
+        nc.sync.dma_start(out=w_scales[64:68, :].bitcast(I32), in_=given_scales[0, 2:6, :])
+        nc.sync.dma_start(out=w_scales[96:100, :].bitcast(I32), in_=given_scales[0, 12:16, :])
+
+        for first_tile in range(LOAD_TILES, TILES, LOAD_TILES):
+            load_edges(first_tile)
+
+        identity = keep.tile([P, P], F32)
+        masks.make_identity(nc, identity[:])
+
+        row_words = rows[:].bitcast(F32)
+
+        triplets = [
+            keep.tile([P, PAIR * P * PACK], BF16, name="triplets%d" % turn, align_bytes=64) for turn in range(2)
+        ]
+        dst_table = keep.tile([DST_P, NODES * GRAPHS * PACK], BF16)
+
+        flipped_of = {}
+        codes_of = {}
+        scales_of = {}
+        sums_of = {}
+        result_of = {}
+
+        def as_words(triplet_rows):
+            return triplet_rows.bitcast(F32).rearrange("p (s c u) -> p s c u", s=PAIR, u=2)
+
+        def transpose_pair(g):
+            turned = flipped.tile([P, PAIR, 2, P], F32)
+            for s in range(PAIR):
+                first_word = (PAIR * g + s) * EDGE_W
+                for u in range(2):
+                    nc.tensor.transpose(
+                        turned[:, s, u, :], row_words[:, first_word + u : first_word + ROW_W : 2], identity[:]
+                    )
+            flipped_of[g] = turned
+
+        def keep_nodes():
+            nodes_t = flipped_of[0]
+            nc.vector.tensor_copy(
+                out=dst_table[:].bitcast(F32).rearrange("p (n b u) -> p n b u", b=GRAPHS, u=2),
+                in_=nodes_t[0:DST_P, 0].rearrange("p u (b n) -> p n b u", b=GRAPHS),
+            )
+            for turn in range(2):
+                nc.vector.tensor_copy(
+                    out=as_words(triplets[turn][0:SRC_END, :]),
+                    in_=nodes_t[0:SRC_END, 0]
+                    .rearrange("p u c -> p c u")
+                    .unsqueeze(1)
+                    .to_broadcast([SRC_END, PAIR, P, 2]),
+                )
+
+        def copy_edges(g):
+            nc.scalar.copy(
+                out=as_words(triplets[g % 2][EDGE_P0:P, :]),
+                in_=flipped_of[g][EDGE_P0:P].rearrange("p s u c -> p s c u"),
+            )
+
+        def spread_dst(g):
+            per_pair = PAIR * GRAPHS * PACK
+            nc.gpsimd.tensor_scalar(
+                out=triplets[g % 2][0:DST_P, :].rearrange("p (q i t) -> p q i t", i=NODES, t=PACK),
+                in0=dst_table[:, g * per_pair : (g + 1) * per_pair]
+                .rearrange("p (q t) -> p q t", t=PACK)
+                .unsqueeze(2)
+                .to_broadcast([DST_P, PAIR * GRAPHS, NODES, PACK]),
+                scalar1=1.0,
+                scalar2=0.0,
+                op0=ALU.mult,
+                op1=ALU.add,
+            )
+
+        def quantise(g):
+            codes = quantised.tile([P, PAIR * P], U32, align_bytes=64)
+            scales = quantised.tile([P, PAIR * P], U8, align_bytes=64)
+            nc.vector.quantize_mx(out=codes[:].bitcast(FP8X4), scales=scales[:], in_=triplets[g % 2][:])
+            codes_of[g] = codes
+            scales_of[g] = scales
+
+        def multiply(g):
+            codes = codes_of[g]
+            scales = scales_of[g]
+            for s in range(PAIR):
+                for h in range(HALVES):
+                    acc = sums.tile([P, BANK], F32)
+                    nc.tensor.matmul_mx(
+                        out=acc[:],
+                        lhsT=codes[:, s * P : (s + 1) * P].bitcast(FP8X4),
+                        lhsT_scale=scales[:, s * P : (s + 1) * P],
+                        rhs=w_codes[:, h * 2 * BANK : (h + 1) * 2 * BANK].bitcast(FP4X4),
+                        rhs_scale=w_scales[:, h * BANK : (h + 1) * BANK],
+                        start=True,
+                        stop=True,
+                    )
+                    sums_of[(g, s, h)] = acc
+
+        def leaky_relu(g, s):
+            if s == 0:
+                result = results.tile([P, PAIR, HID], F32)
+                result_of[g] = result
+            for h in range(HALVES):
+                acc = sums_of[(g, s, h)]
+                part = result_of[g][:, s, h * BANK : (h + 1) * BANK]
+                nc.scalar.copy(out=part, in_=acc[:])
+                nc.vector.scalar_tensor_tensor(
+                    out=part, in0=acc[:], scalar=NEG_SLOPE, in1=part, op0=ALU.mult, op1=ALU.max
+                )
+
+        def store(g):
+            nc.sync.dma_start(
+                out=out_rows[:, g * PAIR * HID : (g + 1) * PAIR * HID],
+                in_=result_of[g][:].rearrange("p s n -> p (s n)"),
+            )
+
+        for step in range(PAIRS + 4):
+            if step < PAIRS:
+                transpose_pair(step)
+            if step == 0:
+                keep_nodes()
+            if step >= 4:
+                leaky_relu(step - 4, 0)
+            if 1 <= step <= PAIRS:
+                copy_edges(step - 1)
+                spread_dst(step - 1)
+            if step >= 4:
+                leaky_relu(step - 4, 1)
+                store(step - 4)
+            if 2 <= step <= PAIRS + 1:
+                quantise(step - 2)
+            if 3 <= step <= PAIRS + 2:
+                multiply(step - 3)

@@ -36,6 +36,7 @@ EDGE_W = EDGE_IN // 2
 FRONT_W = 2 * NODE_W
 ROW_W = P * PACK // 2
 LOAD_TILES = 8
+TURNS = 3
 
 FLOPS = 2 * GRAPHS * NODES * NODES * (2 * NODE_IN + EDGE_IN) * HID
 
@@ -89,7 +90,7 @@ def tile_edge_update_only_pa_t_kernel(tc, node_fts, edge_fts, Wt_words, Wt_scale
         row_words = rows[:].bitcast(F32)
 
         triplets = [
-            keep.tile([P, PAIR * P * PACK], BF16, name="triplets%d" % turn, align_bytes=64) for turn in range(2)
+            keep.tile([P, PAIR * P * PACK], BF16, name="triplets%d" % turn, align_bytes=64) for turn in range(TURNS)
         ]
         dst_table = keep.tile([DST_P, NODES * GRAPHS * PACK], BF16)
 
@@ -118,7 +119,7 @@ def tile_edge_update_only_pa_t_kernel(tc, node_fts, edge_fts, Wt_words, Wt_scale
                 out=dst_table[:].bitcast(F32).rearrange("p (n b u) -> p n b u", b=GRAPHS, u=2),
                 in_=nodes_t[0:DST_P, 0].rearrange("p u (b n) -> p n b u", b=GRAPHS),
             )
-            for turn in range(2):
+            for turn in range(TURNS):
                 nc.vector.tensor_copy(
                     out=as_words(triplets[turn][0:SRC_END, :]),
                     in_=nodes_t[0:SRC_END, 0]
@@ -129,14 +130,14 @@ def tile_edge_update_only_pa_t_kernel(tc, node_fts, edge_fts, Wt_words, Wt_scale
 
         def copy_edges(g):
             nc.scalar.copy(
-                out=as_words(triplets[g % 2][EDGE_P0:P, :]),
+                out=as_words(triplets[g % TURNS][EDGE_P0:P, :]),
                 in_=flipped_of[g][EDGE_P0:P].rearrange("p s u c -> p s c u"),
             )
 
         def spread_dst(g):
             per_pair = PAIR * GRAPHS * PACK
             nc.gpsimd.tensor_scalar(
-                out=triplets[g % 2][0:DST_P, :].rearrange("p (q i t) -> p q i t", i=NODES, t=PACK),
+                out=triplets[g % TURNS][0:DST_P, :].rearrange("p (q i t) -> p q i t", i=NODES, t=PACK),
                 in0=dst_table[:, g * per_pair : (g + 1) * per_pair]
                 .rearrange("p (q t) -> p q t", t=PACK)
                 .unsqueeze(2)
@@ -150,7 +151,7 @@ def tile_edge_update_only_pa_t_kernel(tc, node_fts, edge_fts, Wt_words, Wt_scale
         def quantise(g):
             codes = quantised.tile([P, PAIR * P], U32, align_bytes=64)
             scales = quantised.tile([P, PAIR * P], U8, align_bytes=64)
-            nc.vector.quantize_mx(out=codes[:].bitcast(FP8X4), scales=scales[:], in_=triplets[g % 2][:])
+            nc.vector.quantize_mx(out=codes[:].bitcast(FP8X4), scales=scales[:], in_=triplets[g % TURNS][:])
             codes_of[g] = codes
             scales_of[g] = scales
 

@@ -136,16 +136,12 @@ def tile_edge_update_only_pa_t_kernel(tc, node_fts, edge_fts, Wt_words, Wt_scale
 
         def spread_dst(g):
             per_pair = PAIR * GRAPHS * PACK
-            nc.gpsimd.tensor_scalar(
+            nc.vector.tensor_copy(
                 out=triplets[g % TURNS][0:DST_P, :].rearrange("p (q i t) -> p q i t", i=NODES, t=PACK),
-                in0=dst_table[:, g * per_pair : (g + 1) * per_pair]
+                in_=dst_table[:, g * per_pair : (g + 1) * per_pair]
                 .rearrange("p (q t) -> p q t", t=PACK)
                 .unsqueeze(2)
                 .to_broadcast([DST_P, PAIR * GRAPHS, NODES, PACK]),
-                scalar1=1.0,
-                scalar2=0.0,
-                op0=ALU.mult,
-                op1=ALU.add,
             )
 
         def quantise(g):

@@ -129,19 +129,23 @@ def tile_edge_update_only_pa_t_kernel(tc, node_fts, edge_fts, Wt_words, Wt_scale
                 )
 
         def copy_edges(g):
-            nc.scalar.copy(
+            nc.vector.tensor_copy(
                 out=as_words(triplets[g % TURNS][EDGE_P0:P, :]),
                 in_=flipped_of[g][EDGE_P0:P].rearrange("p s u c -> p s c u"),
             )
 
         def spread_dst(g):
             per_pair = PAIR * GRAPHS * PACK
-            nc.vector.tensor_copy(
+            nc.gpsimd.tensor_scalar(
                 out=triplets[g % TURNS][0:DST_P, :].rearrange("p (q i t) -> p q i t", i=NODES, t=PACK),
-                in_=dst_table[:, g * per_pair : (g + 1) * per_pair]
+                in0=dst_table[:, g * per_pair : (g + 1) * per_pair]
                 .rearrange("p (q t) -> p q t", t=PACK)
                 .unsqueeze(2)
                 .to_broadcast([DST_P, PAIR * GRAPHS, NODES, PACK]),
+                scalar1=1.0,
+                scalar2=0.0,
+                op0=ALU.mult,
+                op1=ALU.add,
             )
 
         def quantise(g):

@@ -37,6 +37,7 @@ FRONT_W = 2 * NODE_W
 ROW_W = P * PACK // 2
 LOAD_TILES = 8
 TURNS = 3
+VECTOR_COPIES_EVERY = 4
 
 FLOPS = 2 * GRAPHS * NODES * NODES * (2 * NODE_IN + EDGE_IN) * HID
 
@@ -51,7 +52,7 @@ def tile_edge_update_only_pa_t_kernel(tc, node_fts, edge_fts, Wt_words, Wt_scale
         ctx.enter_context(tc.manual_schedule())
         keep = ctx.enter_context(tc.tile_pool(name="keep", bufs=1))
         quantised = ctx.enter_context(tc.tile_pool(name="quantised", bufs=3))
-        results = ctx.enter_context(tc.tile_pool(name="results", bufs=4))
+        results = ctx.enter_context(tc.tile_pool(name="results", bufs=8))
         flipped = ctx.enter_context(tc.psum_pool(name="flipped", bufs=2))
         sums = ctx.enter_context(tc.psum_pool(name="sums", bufs=6))
 
@@ -98,7 +99,6 @@ def tile_edge_update_only_pa_t_kernel(tc, node_fts, edge_fts, Wt_words, Wt_scale
         codes_of = {}
         scales_of = {}
         sums_of = {}
-        result_of = {}
 
         def as_words(triplet_rows):
             return triplet_rows.bitcast(F32).rearrange("p (s c u) -> p s c u", s=PAIR, u=2)
@@ -129,10 +129,12 @@ def tile_edge_update_only_pa_t_kernel(tc, node_fts, edge_fts, Wt_words, Wt_scale
                 )
 
         def copy_edges(g):
-            nc.vector.tensor_copy(
-                out=as_words(triplets[g % TURNS][EDGE_P0:P, :]),
-                in_=flipped_of[g][EDGE_P0:P].rearrange("p s u c -> p s c u"),
-            )
+            edges_out = as_words(triplets[g % TURNS][EDGE_P0:P, :])
+            edges_in = flipped_of[g][EDGE_P0:P].rearrange("p s u c -> p s c u")
+            if g % VECTOR_COPIES_EVERY == VECTOR_COPIES_EVERY - 1:
+                nc.vector.tensor_copy(out=edges_out, in_=edges_in)
+            else:
+                nc.scalar.copy(out=edges_out, in_=edges_in)
 
         def spread_dst(g):
             per_pair = PAIR * GRAPHS * PACK
@@ -173,28 +175,24 @@ def tile_edge_update_only_pa_t_kernel(tc, node_fts, edge_fts, Wt_words, Wt_scale
                     sums_of[(g, s, h)] = acc
 
         def leaky_relu(g, s):
-            if s == 0:
-                result = results.tile([P, PAIR, HID], F32)
-                result_of[g] = result
+            result = results.tile([P, HID], F32)
             for h in range(HALVES):
                 acc = sums_of[(g, s, h)]
-                part = result_of[g][:, s, h * BANK : (h + 1) * BANK]
+                part = result[:, h * BANK : (h + 1) * BANK]
                 nc.scalar.copy(out=part, in_=acc[:])
                 nc.vector.scalar_tensor_tensor(
                     out=part, in0=acc[:], scalar=NEG_SLOPE, in1=part, op0=ALU.mult, op1=ALU.max
                 )
-
-        def store(g):
-            nc.sync.dma_start(
-                out=out_rows[:, g * PAIR * HID : (g + 1) * PAIR * HID],
-                in_=result_of[g][:].rearrange("p s n -> p (s n)"),
-            )
+            k = PAIR * g + s
+            nc.sync.dma_start(out=out_rows[:, k * HID : (k + 1) * HID], in_=result[:])
 
         for step in range(PAIRS + 4):
             if step < PAIRS:
                 transpose_pair(step)
             if step == 0:
                 keep_nodes()
+            if 2 <= step <= PAIRS + 1:
+                quantise(step - 2)
             if step >= 4:
                 leaky_relu(step - 4, 0)
             if 1 <= step <= PAIRS:
@@ -202,8 +200,5 @@ def tile_edge_update_only_pa_t_kernel(tc, node_fts, edge_fts, Wt_words, Wt_scale
                 spread_dst(step - 1)
             if step >= 4:
                 leaky_relu(step - 4, 1)
-                store(step - 4)
-            if 2 <= step <= PAIRS + 1:
-                quantise(step - 2)
             if 3 <= step <= PAIRS + 2:
                 multiply(step - 3)

@@ -37,7 +37,7 @@ FRONT_W = 2 * NODE_W
 ROW_W = P * PACK // 2
 LOAD_TILES = 8
 TURNS = 3
-VECTOR_COPIES_EVERY = 4
+VECTOR_COPIES_EVERY = 2
 
 FLOPS = 2 * GRAPHS * NODES * NODES * (2 * NODE_IN + EDGE_IN) * HID
 

@@ -6,7 +6,6 @@ import concourse.mybir as mybir
 F32 = mybir.dt.float32
 BF16 = mybir.dt.bfloat16
 I32 = mybir.dt.int32
-U32 = mybir.dt.uint32
 U8 = mybir.dt.uint8
 FP8X4 = mybir.dt.float8_e4m3fn_x4
 FP4X4 = mybir.dt.float4_e2m1fn_x4
@@ -26,18 +25,20 @@ HALVES = HID // BANK
 TILES = NODES
 PAIR = 2
 PAIRS = TILES // PAIR
+EDGE_P = EDGE_IN // PACK
+GROUP = P // EDGE_P
+BATCH_GROUPS = 2
+BATCH = GROUP * BATCH_GROUPS
+BATCHES = TILES // BATCH
+BATCH_PAIRS = BATCH // PAIR
 
-DST_P = NODE_IN // PACK
-SRC_END = 2 * DST_P
-EDGE_P0 = SRC_END
-
-NODE_W = NODE_IN // 2
+NODE_P = NODE_IN // PACK
+HALF_P = P // 2
 EDGE_W = EDGE_IN // 2
-FRONT_W = 2 * NODE_W
 ROW_W = P * PACK // 2
-LOAD_TILES = 8
 TURNS = 3
-VECTOR_COPIES_EVERY = 2
+NODE_VARIANT = GROUP
+VARIANTS = GROUP + 1
 
 FLOPS = 2 * GRAPHS * NODES * NODES * (2 * NODE_IN + EDGE_IN) * HID
 
@@ -51,126 +52,172 @@ def tile_edge_update_only_pa_t_kernel(tc, node_fts, edge_fts, Wt_words, Wt_scale
     with ExitStack() as ctx:
         ctx.enter_context(tc.manual_schedule())
         keep = ctx.enter_context(tc.tile_pool(name="keep", bufs=1))
-        quantised = ctx.enter_context(tc.tile_pool(name="quantised", bufs=3))
+        packed = ctx.enter_context(tc.tile_pool(name="packed", bufs=2))
+        quantised = ctx.enter_context(tc.tile_pool(name="quantised", bufs=2))
         results = ctx.enter_context(tc.tile_pool(name="results", bufs=8))
-        flipped = ctx.enter_context(tc.psum_pool(name="flipped", bufs=2))
-        sums = ctx.enter_context(tc.psum_pool(name="sums", bufs=6))
+        flipped = ctx.enter_context(tc.psum_pool(name="flipped", bufs=1))
+        sums = ctx.enter_context(tc.psum_pool(name="sums", bufs=7))
 
-        rows = keep.tile([P, 2 * (FRONT_W + TILES * EDGE_W)], BF16)
-        nc.sync.dma_start(out=rows[:, 0:NODE_IN], in_=node_rows)
-        nc.sync.dma_start(out=rows[:, NODE_IN : 2 * NODE_IN], in_=node_rows)
+        front = keep.tile([P, P * PACK], BF16)
+        half = P * PACK // 2
+        nc.vector.memset(front[:, NODE_IN:half], 0.0)
+        nc.vector.memset(front[:, half + NODE_IN : 2 * half], 0.0)
+        nc.sync.dma_start(out=front[:, 0:NODE_IN], in_=node_rows)
+        nc.sync.dma_start(out=front[:, half : half + NODE_IN], in_=node_rows)
 
-        def load_edges(first_tile):
-            first = first_tile * EDGE_IN
-            last = (first_tile + LOAD_TILES) * EDGE_IN
-            nc.sync.dma_start(out=rows[:, 2 * NODE_IN + first : 2 * NODE_IN + last], in_=edge_rows[:, first:last])
+        rows = keep.tile([P, TILES * EDGE_IN], BF16)
+
+        def load_edges(batch):
+            first = batch * BATCH * EDGE_IN
+            last = (batch + 1) * BATCH * EDGE_IN
+            nc.sync.dma_start(out=rows[:, first:last], in_=edge_rows[:, first:last])
 
         load_edges(0)
 
-        w_codes = keep.tile([P, 2 * HID], U8, align_bytes=64)
-        given_words = Wt_words.bitcast(I32)
-        nc.sync.dma_start(out=w_codes[0:DST_P, :].bitcast(I32), in_=given_words[0, DST_P:SRC_END, :])
-        nc.sync.dma_start(out=w_codes[DST_P:SRC_END, :].bitcast(I32), in_=given_words[0, 0:DST_P, :])
-        nc.sync.dma_start(out=w_codes[EDGE_P0:P, :].bitcast(I32), in_=given_words[0, EDGE_P0:P, :])
-
-        w_scales = keep.tile([P, HID], U8, align_bytes=64)
+        w_codes = keep.tile([P, VARIANTS * 2 * HID], U8, align_bytes=64)
+        w_scales = keep.tile([P, VARIANTS * HID], U8, align_bytes=64)
         nc.vector.memset(w_scales[:].bitcast(I32), 0)
+        nc.vector.memset(w_codes[:].bitcast(I32), 0)
+        given_words = Wt_words.bitcast(I32)
         given_scales = Wt_scales.bitcast(I32)
-        nc.sync.dma_start(out=w_scales[0:4, :].bitcast(I32), in_=given_scales[0, 6:10, :])
-        nc.sync.dma_start(out=w_scales[32:34, :].bitcast(I32), in_=given_scales[0, 10:12, :])
-        nc.sync.dma_start(out=w_scales[34:36, :].bitcast(I32), in_=given_scales[0, 0:2, :])
-        nc.sync.dma_start(out=w_scales[64:68, :].bitcast(I32), in_=given_scales[0, 2:6, :])
-        nc.sync.dma_start(out=w_scales[96:100, :].bitcast(I32), in_=given_scales[0, 12:16, :])
 
-        for first_tile in range(LOAD_TILES, TILES, LOAD_TILES):
-            load_edges(first_tile)
+        def load_w(variant, first_p, given_p, count_p):
+            columns = slice(variant * 2 * HID, (variant + 1) * 2 * HID)
+            nc.sync.dma_start(
+                out=w_codes[first_p : first_p + count_p, columns].bitcast(I32),
+                in_=given_words[0, given_p : given_p + count_p, :],
+            )
+            columns = slice(variant * HID, (variant + 1) * HID)
+            done = 0
+            while done < count_p // 8:
+                q = first_p // 8 + done
+                run = min(4 - q % 4, count_p // 8 - done)
+                row = 32 * (q // 4) + q % 4
+                nc.sync.dma_start(
+                    out=w_scales[row : row + run, columns].bitcast(I32),
+                    in_=given_scales[0, given_p // 8 + done : given_p // 8 + done + run, :],
+                )
+                done += run
+
+        load_w(0, 0, 2 * NODE_P, EDGE_P)
+        load_w(NODE_VARIANT, 0, NODE_P, NODE_P)
+        load_w(NODE_VARIANT, HALF_P, 0, NODE_P)
+        for j in range(1, GROUP):
+            load_w(j, j * EDGE_P, 2 * NODE_P, EDGE_P)
+        for batch in range(1, BATCHES):
+            load_edges(batch)
 
         identity = keep.tile([P, P], F32)
         masks.make_identity(nc, identity[:])
 
+        front_words = front[:].bitcast(F32)
+        nodes_t = sums.tile([P, BANK], F32, name="acc")
+        for u in range(2):
+            nc.tensor.transpose(nodes_t[:, u * P : (u + 1) * P], front_words[:, u:ROW_W:2], identity[:])
+        node_values = keep.tile([P, P * PACK], BF16, align_bytes=64)
+        nc.vector.tensor_copy(
+            out=node_values[:].bitcast(F32).rearrange("p (c u) -> p c u", u=2),
+            in_=nodes_t[:, 0 : 2 * P].rearrange("p (u c) -> p c u", u=2),
+        )
+        once_codes = keep.tile([P, P], I32, align_bytes=64)
+        once_scales = keep.tile([P, P], U8, align_bytes=64)
+        nc.vector.memset(once_scales[:].bitcast(I32), 0)
+        nc.vector.quantize_mx(out=once_codes[:].bitcast(FP8X4), scales=once_scales[:], in_=node_values[:])
+        scale_words = keep.tile([P, P * 4], U8)
+        for r in range(4):
+            nc.vector.tensor_copy(out=scale_words[:].rearrange("p (c r) -> p c r", r=4)[:, :, r], in_=once_scales[:])
+
+        slots = TURNS * PAIR
+        node_codes = keep.tile([P, slots * P], I32, align_bytes=64)
+        node_scales = keep.tile([P, slots * P], U8, align_bytes=64)
+        nc.vector.tensor_copy(
+            out=node_codes[HALF_P:P, :].rearrange("p (r c) -> p r c", c=P),
+            in_=once_codes[HALF_P:P, :].unsqueeze(1).to_broadcast([HALF_P, slots, P]),
+        )
+        nc.vector.tensor_copy(
+            out=node_scales[HALF_P:P, :].bitcast(I32).rearrange("p (r w) -> p r w", w=P // 4),
+            in_=once_scales[HALF_P:P, :].bitcast(I32).unsqueeze(1).to_broadcast([HALF_P, slots, P // 4]),
+        )
+
+        def spread_dst(g):
+            columns = slice((g % TURNS) * PAIR * P, (g % TURNS + 1) * PAIR * P)
+            nc.gpsimd.tensor_copy(
+                out=node_codes[0:HALF_P, columns].rearrange("p (s b i) -> p s b i", s=PAIR, b=GRAPHS),
+                in_=once_codes[0:HALF_P, :]
+                .rearrange("p (b n) -> p n b", b=GRAPHS)[:, PAIR * g : PAIR * (g + 1), :]
+                .unsqueeze(3)
+                .to_broadcast([HALF_P, PAIR, GRAPHS, NODES]),
+            )
+            nc.gpsimd.tensor_copy(
+                out=node_scales[0:HALF_P, columns].bitcast(I32).rearrange("p (s b w) -> p s b w", s=PAIR, b=GRAPHS),
+                in_=scale_words[0:HALF_P, :]
+                .bitcast(I32)
+                .rearrange("p (b n) -> p n b", b=GRAPHS)[:, PAIR * g : PAIR * (g + 1), :]
+                .unsqueeze(3)
+                .to_broadcast([HALF_P, PAIR, GRAPHS, NODES // 4]),
+            )
+
         row_words = rows[:].bitcast(F32)
-
-        triplets = [
-            keep.tile([P, PAIR * P * PACK], BF16, name="triplets%d" % turn, align_bytes=64) for turn in range(TURNS)
-        ]
-        dst_table = keep.tile([DST_P, NODES * GRAPHS * PACK], BF16)
-
         flipped_of = {}
+        values_of = {}
         codes_of = {}
         scales_of = {}
         sums_of = {}
 
-        def as_words(triplet_rows):
-            return triplet_rows.bitcast(F32).rearrange("p (s c u) -> p s c u", s=PAIR, u=2)
-
-        def transpose_pair(g):
-            turned = flipped.tile([P, PAIR, 2, P], F32)
-            for s in range(PAIR):
-                first_word = (PAIR * g + s) * EDGE_W
+        def transpose_batch(batch):
+            turned = flipped.tile([P, BATCH_GROUPS, 2, P], F32)
+            for q in range(BATCH_GROUPS):
+                first_word = (batch * BATCH + q * GROUP) * EDGE_W
                 for u in range(2):
                     nc.tensor.transpose(
-                        turned[:, s, u, :], row_words[:, first_word + u : first_word + ROW_W : 2], identity[:]
+                        turned[:, q, u, :], row_words[:, first_word + u : first_word + ROW_W : 2], identity[:]
                     )
-            flipped_of[g] = turned
+            flipped_of[batch] = turned
 
-        def keep_nodes():
-            nodes_t = flipped_of[0]
-            nc.vector.tensor_copy(
-                out=dst_table[:].bitcast(F32).rearrange("p (n b u) -> p n b u", b=GRAPHS, u=2),
-                in_=nodes_t[0:DST_P, 0].rearrange("p u (b n) -> p n b u", b=GRAPHS),
+        def copy_batch(batch):
+            values = packed.tile([P, BATCH_GROUPS * P * PACK], BF16, align_bytes=64)
+            nc.scalar.copy(
+                out=values[:].bitcast(F32).rearrange("p (q c u) -> p q c u", q=BATCH_GROUPS, u=2),
+                in_=flipped_of[batch][:].rearrange("p q u c -> p q c u"),
             )
-            for turn in range(TURNS):
-                nc.vector.tensor_copy(
-                    out=as_words(triplets[turn][0:SRC_END, :]),
-                    in_=nodes_t[0:SRC_END, 0]
-                    .rearrange("p u c -> p c u")
-                    .unsqueeze(1)
-                    .to_broadcast([SRC_END, PAIR, P, 2]),
-                )
+            values_of[batch] = values
 
-        def copy_edges(g):
-            edges_out = as_words(triplets[g % TURNS][EDGE_P0:P, :])
-            edges_in = flipped_of[g][EDGE_P0:P].rearrange("p s u c -> p s c u")
-            if g % VECTOR_COPIES_EVERY == VECTOR_COPIES_EVERY - 1:
-                nc.vector.tensor_copy(out=edges_out, in_=edges_in)
-            else:
-                nc.scalar.copy(out=edges_out, in_=edges_in)
+        def quantise_batch(batch):
+            codes = quantised.tile([P, BATCH_GROUPS * P], I32, align_bytes=64)
+            scales = quantised.tile([P, BATCH_GROUPS * P], U8, align_bytes=64)
+            nc.vector.quantize_mx(out=codes[:].bitcast(FP8X4), scales=scales[:], in_=values_of[batch][:])
+            codes_of[batch] = codes
+            scales_of[batch] = scales
 
-        def spread_dst(g):
-            per_pair = PAIR * GRAPHS * PACK
-            nc.gpsimd.tensor_scalar(
-                out=triplets[g % TURNS][0:DST_P, :].rearrange("p (q i t) -> p q i t", i=NODES, t=PACK),
-                in0=dst_table[:, g * per_pair : (g + 1) * per_pair]
-                .rearrange("p (q t) -> p q t", t=PACK)
-                .unsqueeze(2)
-                .to_broadcast([DST_P, PAIR * GRAPHS, NODES, PACK]),
-                scalar1=1.0,
-                scalar2=0.0,
-                op0=ALU.mult,
-                op1=ALU.add,
+        def w_operands(variant, h):
+            return dict(
+                rhs=w_codes[:, (variant * HALVES + h) * 2 * BANK : (variant * HALVES + h + 1) * 2 * BANK].bitcast(FP4X4),
+                rhs_scale=w_scales[:, (variant * HALVES + h) * BANK : (variant * HALVES + h + 1) * BANK],
             )
-
-        def quantise(g):
-            codes = quantised.tile([P, PAIR * P], U32, align_bytes=64)
-            scales = quantised.tile([P, PAIR * P], U8, align_bytes=64)
-            nc.vector.quantize_mx(out=codes[:].bitcast(FP8X4), scales=scales[:], in_=triplets[g % TURNS][:])
-            codes_of[g] = codes
-            scales_of[g] = scales
 
         def multiply(g):
-            codes = codes_of[g]
-            scales = scales_of[g]
             for s in range(PAIR):
+                k = PAIR * g + s
+                batch = k // BATCH
+                group_columns = slice((k % BATCH) // GROUP * P, ((k % BATCH) // GROUP + 1) * P)
+                node_columns = slice(((g % TURNS) * PAIR + s) * P, ((g % TURNS) * PAIR + s + 1) * P)
                 for h in range(HALVES):
                     acc = sums.tile([P, BANK], F32)
                     nc.tensor.matmul_mx(
                         out=acc[:],
-                        lhsT=codes[:, s * P : (s + 1) * P].bitcast(FP8X4),
-                        lhsT_scale=scales[:, s * P : (s + 1) * P],
-                        rhs=w_codes[:, h * 2 * BANK : (h + 1) * 2 * BANK].bitcast(FP4X4),
-                        rhs_scale=w_scales[:, h * BANK : (h + 1) * BANK],
+                        lhsT=codes_of[batch][:, group_columns].bitcast(FP8X4),
+                        lhsT_scale=scales_of[batch][:, group_columns],
                         start=True,
+                        stop=False,
+                        **w_operands(k % GROUP, h),
+                    )
+                    nc.tensor.matmul_mx(
+                        out=acc[:],
+                        lhsT=node_codes[:, node_columns].bitcast(FP8X4),
+                        lhsT_scale=node_scales[:, node_columns],
+                        start=False,
                         stop=True,
+                        **w_operands(NODE_VARIANT, h),
                     )
                     sums_of[(g, s, h)] = acc
 
@@ -186,19 +233,24 @@ def tile_edge_update_only_pa_t_kernel(tc, node_fts, edge_fts, Wt_words, Wt_scale
             k = PAIR * g + s
             nc.sync.dma_start(out=out_rows[:, k * HID : (k + 1) * HID], in_=result[:])
 
-        for step in range(PAIRS + 4):
+        transpose_batch(0)
+        copy_batch(0)
+        quantise_batch(0)
+        spread_dst(0)
+        spread_dst(1)
+        for step in range(PAIRS + 1):
+            ahead = step // BATCH_PAIRS + 1
+            if ahead < BATCHES and step % BATCH_PAIRS == 0:
+                transpose_batch(ahead)
+            if ahead < BATCHES and step % BATCH_PAIRS == 2:
+                quantise_batch(ahead)
+            if step >= 1:
+                leaky_relu(step - 1, 0)
+            if ahead < BATCHES and step % BATCH_PAIRS == 1:
+                copy_batch(ahead)
+            if step + 2 < PAIRS:
+                spread_dst(step + 2)
+            if step >= 1:
+                leaky_relu(step - 1, 1)
             if step < PAIRS:
-                transpose_pair(step)
-            if step == 0:
-                keep_nodes()
-            if 2 <= step <= PAIRS + 1:
-                quantise(step - 2)
-            if step >= 4:
-                leaky_relu(step - 4, 0)
-            if 1 <= step <= PAIRS:
-                copy_edges(step - 1)
-                spread_dst(step - 1)
-            if step >= 4:
-                leaky_relu(step - 4, 1)
-            if 3 <= step <= PAIRS + 2:
-                multiply(step - 3)
+                multiply(step)

@@ -77,7 +77,7 @@ def tile_edge_update_only_pa_t_kernel(tc, node_fts, edge_fts, Wt_words, Wt_scale
         w_codes = keep.tile([P, VARIANTS * 2 * HID], U8, align_bytes=64)
         w_scales = keep.tile([P, VARIANTS * HID], U8, align_bytes=64)
         nc.vector.memset(w_scales[:].bitcast(I32), 0)
-        nc.vector.memset(w_codes[:].bitcast(I32), 0)
+        nc.vector.memset(w_codes[:, 0 : 2 * HID].bitcast(I32), 0)
         given_words = Wt_words.bitcast(I32)
         given_scales = Wt_scales.bitcast(I32)
 
@@ -99,9 +99,10 @@ def tile_edge_update_only_pa_t_kernel(tc, node_fts, edge_fts, Wt_words, Wt_scale
                 )
                 done += run
 
+        load_w(NODE_VARIANT, 0, NODE_P, HALF_P)
+        load_w(NODE_VARIANT, HALF_P, 0, HALF_P)
         load_w(0, 0, 2 * NODE_P, EDGE_P)
-        load_w(NODE_VARIANT, 0, NODE_P, NODE_P)
-        load_w(NODE_VARIANT, HALF_P, 0, NODE_P)
+        nc.vector.memset(w_codes[:, 2 * HID : GROUP * 2 * HID].bitcast(I32), 0)
         for j in range(1, GROUP):
             load_w(j, j * EDGE_P, 2 * NODE_P, EDGE_P)
         for batch in range(1, BATCHES):
@@ -130,25 +131,31 @@ def tile_edge_update_only_pa_t_kernel(tc, node_fts, edge_fts, Wt_words, Wt_scale
         slots = TURNS * PAIR
         node_codes = keep.tile([P, slots * P], I32, align_bytes=64)
         node_scales = keep.tile([P, slots * P], U8, align_bytes=64)
-        nc.vector.tensor_copy(
-            out=node_codes[HALF_P:P, :].rearrange("p (r c) -> p r c", c=P),
-            in_=once_codes[HALF_P:P, :].unsqueeze(1).to_broadcast([HALF_P, slots, P]),
-        )
-        nc.vector.tensor_copy(
-            out=node_scales[HALF_P:P, :].bitcast(I32).rearrange("p (r w) -> p r w", w=P // 4),
-            in_=once_scales[HALF_P:P, :].bitcast(I32).unsqueeze(1).to_broadcast([HALF_P, slots, P // 4]),
-        )
 
-        def spread_dst(g):
+        def keep_src(first_slot, last_slot):
+            count = last_slot - first_slot
+            nc.vector.tensor_copy(
+                out=node_scales[HALF_P:P, first_slot * P : last_slot * P].bitcast(I32).rearrange("p (r w) -> p r w", r=count),
+                in_=once_scales[HALF_P:P, :].bitcast(I32).unsqueeze(1).to_broadcast([HALF_P, count, P // 4]),
+            )
+            nc.vector.tensor_copy(
+                out=node_codes[HALF_P:P, first_slot * P : last_slot * P].rearrange("p (r c) -> p r c", r=count),
+                in_=once_codes[HALF_P:P, :].unsqueeze(1).to_broadcast([HALF_P, count, P]),
+            )
+
+        def spread_codes(engine, g):
             columns = slice((g % TURNS) * PAIR * P, (g % TURNS + 1) * PAIR * P)
-            nc.gpsimd.tensor_copy(
+            engine.tensor_copy(
                 out=node_codes[0:HALF_P, columns].rearrange("p (s b i) -> p s b i", s=PAIR, b=GRAPHS),
                 in_=once_codes[0:HALF_P, :]
                 .rearrange("p (b n) -> p n b", b=GRAPHS)[:, PAIR * g : PAIR * (g + 1), :]
                 .unsqueeze(3)
                 .to_broadcast([HALF_P, PAIR, GRAPHS, NODES]),
             )
-            nc.gpsimd.tensor_copy(
+
+        def spread_scales(engine, g):
+            columns = slice((g % TURNS) * PAIR * P, (g % TURNS + 1) * PAIR * P)
+            engine.tensor_copy(
                 out=node_scales[0:HALF_P, columns].bitcast(I32).rearrange("p (s b w) -> p s b w", s=PAIR, b=GRAPHS),
                 in_=scale_words[0:HALF_P, :]
                 .bitcast(I32)
@@ -156,6 +163,10 @@ def tile_edge_update_only_pa_t_kernel(tc, node_fts, edge_fts, Wt_words, Wt_scale
                 .unsqueeze(3)
                 .to_broadcast([HALF_P, PAIR, GRAPHS, NODES // 4]),
             )
+
+        def spread_dst(g):
+            spread_codes(nc.gpsimd, g)
+            spread_scales(nc.gpsimd, g)
 
         row_words = rows[:].bitcast(F32)
         flipped_of = {}
@@ -235,8 +246,11 @@ def tile_edge_update_only_pa_t_kernel(tc, node_fts, edge_fts, Wt_words, Wt_scale
 
         transpose_batch(0)
         copy_batch(0)
+        spread_codes(nc.gpsimd, 0)
+        spread_scales(nc.vector, 0)
+        keep_src(0, PAIR)
         quantise_batch(0)
-        spread_dst(0)
+        keep_src(PAIR, slots)
         spread_dst(1)
         for step in range(PAIRS + 1):
             ahead = step // BATCH_PAIRS + 1

@@ -256,10 +256,10 @@ def tile_edge_update_only_pa_t_kernel(tc, node_fts, edge_fts, Wt_words, Wt_scale
             ahead = step // BATCH_PAIRS + 1
             if ahead < BATCHES and step % BATCH_PAIRS == 0:
                 transpose_batch(ahead)
-            if ahead < BATCHES and step % BATCH_PAIRS == 2:
-                quantise_batch(ahead)
             if step >= 1:
                 leaky_relu(step - 1, 0)
+            if ahead < BATCHES and step % BATCH_PAIRS == 2:
+                quantise_batch(ahead)
             if ahead < BATCHES and step % BATCH_PAIRS == 1:
                 copy_batch(ahead)
             if step + 2 < PAIRS:

@@ -73,6 +73,7 @@ def tile_edge_update_only_pa_t_kernel(tc, node_fts, edge_fts, Wt_words, Wt_scale
             nc.sync.dma_start(out=rows[:, first:last], in_=edge_rows[:, first:last])
 
         load_edges(0)
+        load_edges(1)
 
         w_codes = keep.tile([P, VARIANTS * 2 * HID], U8, align_bytes=64)
         w_scales = keep.tile([P, VARIANTS * HID], U8, align_bytes=64)
@@ -105,7 +106,7 @@ def tile_edge_update_only_pa_t_kernel(tc, node_fts, edge_fts, Wt_words, Wt_scale
         nc.vector.memset(w_codes[:, 2 * HID : GROUP * 2 * HID].bitcast(I32), 0)
         for j in range(1, GROUP):
             load_w(j, j * EDGE_P, 2 * NODE_P, EDGE_P)
-        for batch in range(1, BATCHES):
+        for batch in range(2, BATCHES):
             load_edges(batch)
 
         identity = keep.tile([P, P], F32)

@@ -33,12 +33,14 @@ BATCHES = TILES // BATCH
 BATCH_PAIRS = BATCH // PAIR
 
 NODE_P = NODE_IN // PACK
-HALF_P = P // 2
+EDGES_AT = 2 * NODE_P
+SCALE_P = 34
+SCALE_ROWS = 4
 EDGE_W = EDGE_IN // 2
 ROW_W = P * PACK // 2
-TURNS = 3
-NODE_VARIANT = GROUP
-VARIANTS = GROUP + 1
+TURNS = BATCH // PAIR
+WHOLE = GROUP - 1
+VARIANTS = GROUP
 
 FLOPS = 2 * GRAPHS * NODES * NODES * (2 * NODE_IN + EDGE_IN) * HID
 
@@ -55,15 +57,12 @@ def tile_edge_update_only_pa_t_kernel(tc, node_fts, edge_fts, Wt_words, Wt_scale
         packed = ctx.enter_context(tc.tile_pool(name="packed", bufs=2))
         quantised = ctx.enter_context(tc.tile_pool(name="quantised", bufs=2))
         results = ctx.enter_context(tc.tile_pool(name="results", bufs=8))
-        flipped = ctx.enter_context(tc.psum_pool(name="flipped", bufs=1))
-        sums = ctx.enter_context(tc.psum_pool(name="sums", bufs=7))
+        sums = ctx.enter_context(tc.psum_pool(name="sums", bufs=8))
 
         front = keep.tile([P, P * PACK], BF16)
-        half = P * PACK // 2
-        nc.vector.memset(front[:, NODE_IN:half], 0.0)
-        nc.vector.memset(front[:, half + NODE_IN : 2 * half], 0.0)
+        nc.vector.memset(front[:, 2 * NODE_IN :], 0.0)
         nc.sync.dma_start(out=front[:, 0:NODE_IN], in_=node_rows)
-        nc.sync.dma_start(out=front[:, half : half + NODE_IN], in_=node_rows)
+        nc.sync.dma_start(out=front[:, NODE_IN : 2 * NODE_IN], in_=node_rows)
 
         rows = keep.tile([P, TILES * EDGE_IN], BF16)
 
@@ -100,12 +99,15 @@ def tile_edge_update_only_pa_t_kernel(tc, node_fts, edge_fts, Wt_words, Wt_scale
                 )
                 done += run
 
-        load_w(NODE_VARIANT, 0, NODE_P, HALF_P)
-        load_w(NODE_VARIANT, HALF_P, 0, HALF_P)
-        load_w(0, 0, 2 * NODE_P, EDGE_P)
-        nc.vector.memset(w_codes[:, 2 * HID : GROUP * 2 * HID].bitcast(I32), 0)
-        for j in range(1, GROUP):
-            load_w(j, j * EDGE_P, 2 * NODE_P, EDGE_P)
+        load_w(WHOLE, 0, NODE_P, 32)
+        load_w(WHOLE, 32, NODE_P + 32, 16)
+        load_w(WHOLE, NODE_P, 0, 16)
+        load_w(WHOLE, 64, 16, 32)
+        load_w(WHOLE, EDGES_AT, EDGES_AT, EDGE_P)
+        load_w(0, 0, EDGES_AT, EDGE_P)
+        nc.vector.memset(w_codes[:, 2 * HID : WHOLE * 2 * HID].bitcast(I32), 0)
+        for j in range(1, WHOLE):
+            load_w(j, j * EDGE_P, EDGES_AT, EDGE_P)
         for batch in range(2, BATCHES):
             load_edges(batch)
 
@@ -136,38 +138,50 @@ def tile_edge_update_only_pa_t_kernel(tc, node_fts, edge_fts, Wt_words, Wt_scale
         def keep_src(first_slot, last_slot):
             count = last_slot - first_slot
             nc.vector.tensor_copy(
-                out=node_scales[HALF_P:P, first_slot * P : last_slot * P].bitcast(I32).rearrange("p (r w) -> p r w", r=count),
-                in_=once_scales[HALF_P:P, :].bitcast(I32).unsqueeze(1).to_broadcast([HALF_P, count, P // 4]),
+                out=node_codes[:, first_slot * P : last_slot * P].rearrange("p (r c) -> p r c", r=count),
+                in_=once_codes[:].unsqueeze(1).to_broadcast([P, count, P]),
             )
             nc.vector.tensor_copy(
-                out=node_codes[HALF_P:P, first_slot * P : last_slot * P].rearrange("p (r c) -> p r c", r=count),
-                in_=once_codes[HALF_P:P, :].unsqueeze(1).to_broadcast([HALF_P, count, P]),
+                out=node_scales[:, first_slot * P : last_slot * P].bitcast(I32).rearrange("p (r w) -> p r w", r=count),
+                in_=once_scales[:].bitcast(I32).unsqueeze(1).to_broadcast([P, count, P // 4]),
             )
 
         def spread_codes(engine, g):
             columns = slice((g % TURNS) * PAIR * P, (g % TURNS + 1) * PAIR * P)
             engine.tensor_copy(
-                out=node_codes[0:HALF_P, columns].rearrange("p (s b i) -> p s b i", s=PAIR, b=GRAPHS),
-                in_=once_codes[0:HALF_P, :]
+                out=node_codes[0:NODE_P, columns].rearrange("p (s b i) -> p s b i", s=PAIR, b=GRAPHS),
+                in_=once_codes[0:NODE_P, :]
                 .rearrange("p (b n) -> p n b", b=GRAPHS)[:, PAIR * g : PAIR * (g + 1), :]
                 .unsqueeze(3)
-                .to_broadcast([HALF_P, PAIR, GRAPHS, NODES]),
+                .to_broadcast([NODE_P, PAIR, GRAPHS, NODES]),
             )
 
         def spread_scales(engine, g):
             columns = slice((g % TURNS) * PAIR * P, (g % TURNS + 1) * PAIR * P)
             engine.tensor_copy(
-                out=node_scales[0:HALF_P, columns].bitcast(I32).rearrange("p (s b w) -> p s b w", s=PAIR, b=GRAPHS),
-                in_=scale_words[0:HALF_P, :]
+                out=node_scales[0:SCALE_P, columns].bitcast(I32).rearrange("p (s b w) -> p s b w", s=PAIR, b=GRAPHS),
+                in_=scale_words[0:SCALE_P, :]
                 .bitcast(I32)
                 .rearrange("p (b n) -> p n b", b=GRAPHS)[:, PAIR * g : PAIR * (g + 1), :]
                 .unsqueeze(3)
-                .to_broadcast([HALF_P, PAIR, GRAPHS, NODES // 4]),
+                .to_broadcast([SCALE_P, PAIR, GRAPHS, NODES // 4]),
             )
 
         def spread_dst(g):
             spread_codes(nc.gpsimd, g)
             spread_scales(nc.gpsimd, g)
+            if (PAIR * g + 1) % GROUP == WHOLE:
+                place_edges(PAIR * g + 1)
+
+        def place_edges(k):
+            batch = k // BATCH
+            source = slice((k % BATCH) // GROUP * P, ((k % BATCH) // GROUP + 1) * P)
+            slot = slice(k % slots * P, (k % slots + 1) * P)
+            nc.gpsimd.tensor_copy(out=node_codes[EDGES_AT:P, slot], in_=codes_of[batch][EDGES_AT:P, source])
+            live = slice(EDGES_AT, EDGES_AT + SCALE_ROWS)
+            nc.gpsimd.tensor_copy(
+                out=node_scales[live, slot].bitcast(I32), in_=scales_of[batch][live, source].bitcast(I32)
+            )
 
         row_words = rows[:].bitcast(F32)
         flipped_of = {}
@@ -177,7 +191,7 @@ def tile_edge_update_only_pa_t_kernel(tc, node_fts, edge_fts, Wt_words, Wt_scale
         sums_of = {}
 
         def transpose_batch(batch):
-            turned = flipped.tile([P, BATCH_GROUPS, 2, P], F32)
+            turned = sums.tile([P, BATCH_GROUPS, 2, P], F32, name="acc")
             for q in range(BATCH_GROUPS):
                 first_word = (batch * BATCH + q * GROUP) * EDGE_W
                 for u in range(2):
@@ -215,21 +229,22 @@ def tile_edge_update_only_pa_t_kernel(tc, node_fts, edge_fts, Wt_words, Wt_scale
                 node_columns = slice(((g % TURNS) * PAIR + s) * P, ((g % TURNS) * PAIR + s + 1) * P)
                 for h in range(HALVES):
                     acc = sums.tile([P, BANK], F32)
-                    nc.tensor.matmul_mx(
-                        out=acc[:],
-                        lhsT=codes_of[batch][:, group_columns].bitcast(FP8X4),
-                        lhsT_scale=scales_of[batch][:, group_columns],
-                        start=True,
-                        stop=False,
-                        **w_operands(k % GROUP, h),
-                    )
+                    if k % GROUP != WHOLE:
+                        nc.tensor.matmul_mx(
+                            out=acc[:],
+                            lhsT=codes_of[batch][:, group_columns].bitcast(FP8X4),
+                            lhsT_scale=scales_of[batch][:, group_columns],
+                            start=True,
+                            stop=False,
+                            **w_operands(k % GROUP, h),
+                        )
                     nc.tensor.matmul_mx(
                         out=acc[:],
                         lhsT=node_codes[:, node_columns].bitcast(FP8X4),
                         lhsT_scale=node_scales[:, node_columns],
-                        start=False,
+                        start=k % GROUP == WHOLE,
                         stop=True,
-                        **w_operands(NODE_VARIANT, h),
+                        **w_operands(WHOLE, h),
                     )
                     sums_of[(g, s, h)] = acc
 
@@ -247,9 +262,9 @@ def tile_edge_update_only_pa_t_kernel(tc, node_fts, edge_fts, Wt_words, Wt_scale
 
         transpose_batch(0)
         copy_batch(0)
+        keep_src(0, PAIR)
         spread_codes(nc.gpsimd, 0)
         spread_scales(nc.vector, 0)
-        keep_src(0, PAIR)
         quantise_batch(0)
         keep_src(PAIR, slots)
         spread_dst(1)

from contextlib import ExitStack

import concourse.masks as masks
import concourse.mybir as mybir

F32 = mybir.dt.float32
BF16 = mybir.dt.bfloat16
I32 = mybir.dt.int32
U8 = mybir.dt.uint8
FP8X4 = mybir.dt.float8_e4m3fn_x4
FP4X4 = mybir.dt.float4_e2m1fn_x4
ALU = mybir.AluOpType

P = 128
PACK = 4
GRAPHS = 2
NODES = 64
NODE_IN = 192
EDGE_IN = 128
HID = 1024
NEG_SLOPE = 0.1
BANK = 512
HALVES = HID // BANK

TILES = NODES
PAIR = 2
PAIRS = TILES // PAIR
EDGE_P = EDGE_IN // PACK
GROUP = P // EDGE_P
BATCH_GROUPS = 2
BATCH = GROUP * BATCH_GROUPS
BATCHES = TILES // BATCH
BATCH_PAIRS = BATCH // PAIR

NODE_P = NODE_IN // PACK
EDGES_AT = 2 * NODE_P
SCALE_P = 34
SCALE_ROWS = 4
EDGE_W = EDGE_IN // 2
ROW_W = P * PACK // 2
TURNS = BATCH // PAIR
WHOLE = GROUP - 1
VARIANTS = GROUP

FLOPS = 2 * GRAPHS * NODES * NODES * (2 * NODE_IN + EDGE_IN) * HID


def tile_edge_update_only_pa_t_kernel(tc, node_fts, edge_fts, Wt_words, Wt_scales, out):
    nc = tc.nc
    node_rows = node_fts.rearrange("b n f -> (b n) f")
    edge_rows = edge_fts.rearrange("b (i k) f -> (b i) (k f)", k=NODES)
    out_rows = out.rearrange("b (i k) n -> (b i) (k n)", k=NODES)

    with ExitStack() as ctx:
        ctx.enter_context(tc.manual_schedule())
        keep = ctx.enter_context(tc.tile_pool(name="keep", bufs=1))
        packed = ctx.enter_context(tc.tile_pool(name="packed", bufs=2))
        quantised = ctx.enter_context(tc.tile_pool(name="quantised", bufs=2))
        results = ctx.enter_context(tc.tile_pool(name="results", bufs=8))
        sums = ctx.enter_context(tc.psum_pool(name="sums", bufs=8))

        front = keep.tile([P, P * PACK], BF16)
        nc.vector.memset(front[:, 2 * NODE_IN :], 0.0)
        nc.sync.dma_start(out=front[:, 0:NODE_IN], in_=node_rows)
        nc.sync.dma_start(out=front[:, NODE_IN : 2 * NODE_IN], in_=node_rows)

        rows = keep.tile([P, TILES * EDGE_IN], BF16)

        def load_edges(batch):
            first = batch * BATCH * EDGE_IN
            last = (batch + 1) * BATCH * EDGE_IN
            nc.sync.dma_start(out=rows[:, first:last], in_=edge_rows[:, first:last])

        load_edges(0)
        load_edges(1)

        w_codes = keep.tile([P, VARIANTS * 2 * HID], U8, align_bytes=64)
        w_scales = keep.tile([P, VARIANTS * HID], U8, align_bytes=64)
        nc.vector.memset(w_scales[:].bitcast(I32), 0)
        nc.vector.memset(w_codes[:, 0 : 2 * HID].bitcast(I32), 0)
        given_words = Wt_words.bitcast(I32)
        given_scales = Wt_scales.bitcast(I32)

        def load_w(variant, first_p, given_p, count_p):
            columns = slice(variant * 2 * HID, (variant + 1) * 2 * HID)
            nc.sync.dma_start(
                out=w_codes[first_p : first_p + count_p, columns].bitcast(I32),
                in_=given_words[0, given_p : given_p + count_p, :],
            )
            columns = slice(variant * HID, (variant + 1) * HID)
            done = 0
            while done < count_p // 8:
                q = first_p // 8 + done
                run = min(4 - q % 4, count_p // 8 - done)
                row = 32 * (q // 4) + q % 4
                nc.sync.dma_start(
                    out=w_scales[row : row + run, columns].bitcast(I32),
                    in_=given_scales[0, given_p // 8 + done : given_p // 8 + done + run, :],
                )
                done += run

        load_w(WHOLE, 0, NODE_P, 32)
        load_w(WHOLE, 32, NODE_P + 32, 16)
        load_w(WHOLE, NODE_P, 0, 16)
        load_w(WHOLE, 64, 16, 32)
        load_w(WHOLE, EDGES_AT, EDGES_AT, EDGE_P)
        load_w(0, 0, EDGES_AT, EDGE_P)
        nc.vector.memset(w_codes[:, 2 * HID : WHOLE * 2 * HID].bitcast(I32), 0)
        for j in range(1, WHOLE):
            load_w(j, j * EDGE_P, EDGES_AT, EDGE_P)
        for batch in range(2, BATCHES):
            load_edges(batch)

        identity = keep.tile([P, P], F32)
        masks.make_identity(nc, identity[:])

        front_words = front[:].bitcast(F32)
        nodes_t = sums.tile([P, BANK], F32, name="acc")
        for u in range(2):
            nc.tensor.transpose(nodes_t[:, u * P : (u + 1) * P], front_words[:, u:ROW_W:2], identity[:])
        node_values = keep.tile([P, P * PACK], BF16, align_bytes=64)
        nc.vector.tensor_copy(
            out=node_values[:].bitcast(F32).rearrange("p (c u) -> p c u", u=2),
            in_=nodes_t[:, 0 : 2 * P].rearrange("p (u c) -> p c u", u=2),
        )
        once_codes = keep.tile([P, P], I32, align_bytes=64)
        once_scales = keep.tile([P, P], U8, align_bytes=64)
        nc.vector.memset(once_scales[:].bitcast(I32), 0)
        nc.vector.quantize_mx(out=once_codes[:].bitcast(FP8X4), scales=once_scales[:], in_=node_values[:])
        scale_words = keep.tile([P, P * 4], U8)
        for r in range(4):
            nc.vector.tensor_copy(out=scale_words[:].rearrange("p (c r) -> p c r", r=4)[:, :, r], in_=once_scales[:])

        slots = TURNS * PAIR
        node_codes = keep.tile([P, slots * P], I32, align_bytes=64)
        node_scales = keep.tile([P, slots * P], U8, align_bytes=64)

        def keep_src(first_slot, last_slot):
            count = last_slot - first_slot
            nc.vector.tensor_copy(
                out=node_codes[:, first_slot * P : last_slot * P].rearrange("p (r c) -> p r c", r=count),
                in_=once_codes[:].unsqueeze(1).to_broadcast([P, count, P]),
            )
            nc.vector.tensor_copy(
                out=node_scales[:, first_slot * P : last_slot * P].bitcast(I32).rearrange("p (r w) -> p r w", r=count),
                in_=once_scales[:].bitcast(I32).unsqueeze(1).to_broadcast([P, count, P // 4]),
            )

        def spread_codes(engine, g):
            columns = slice((g % TURNS) * PAIR * P, (g % TURNS + 1) * PAIR * P)
            engine.tensor_copy(
                out=node_codes[0:NODE_P, columns].rearrange("p (s b i) -> p s b i", s=PAIR, b=GRAPHS),
                in_=once_codes[0:NODE_P, :]
                .rearrange("p (b n) -> p n b", b=GRAPHS)[:, PAIR * g : PAIR * (g + 1), :]
                .unsqueeze(3)
                .to_broadcast([NODE_P, PAIR, GRAPHS, NODES]),
            )

        def spread_scales(engine, g):
            columns = slice((g % TURNS) * PAIR * P, (g % TURNS + 1) * PAIR * P)
            engine.tensor_copy(
                out=node_scales[0:SCALE_P, columns].bitcast(I32).rearrange("p (s b w) -> p s b w", s=PAIR, b=GRAPHS),
                in_=scale_words[0:SCALE_P, :]
                .bitcast(I32)
                .rearrange("p (b n) -> p n b", b=GRAPHS)[:, PAIR * g : PAIR * (g + 1), :]
                .unsqueeze(3)
                .to_broadcast([SCALE_P, PAIR, GRAPHS, NODES // 4]),
            )

        def spread_dst(g):
            spread_codes(nc.gpsimd, g)
            spread_scales(nc.gpsimd, g)
            if (PAIR * g + 1) % GROUP == WHOLE:
                place_edges(PAIR * g + 1)

        def place_edges(k):
            batch = k // BATCH
            source = slice((k % BATCH) // GROUP * P, ((k % BATCH) // GROUP + 1) * P)
            slot = slice(k % slots * P, (k % slots + 1) * P)
            nc.gpsimd.tensor_copy(out=node_codes[EDGES_AT:P, slot], in_=codes_of[batch][EDGES_AT:P, source])
            live = slice(EDGES_AT, EDGES_AT + SCALE_ROWS)
            nc.gpsimd.tensor_copy(
                out=node_scales[live, slot].bitcast(I32), in_=scales_of[batch][live, source].bitcast(I32)
            )

        row_words = rows[:].bitcast(F32)
        flipped_of = {}
        values_of = {}
        codes_of = {}
        scales_of = {}
        sums_of = {}

        def transpose_batch(batch):
            turned = sums.tile([P, BATCH_GROUPS, 2, P], F32, name="acc")
            for q in range(BATCH_GROUPS):
                first_word = (batch * BATCH + q * GROUP) * EDGE_W
                for u in range(2):
                    nc.tensor.transpose(
                        turned[:, q, u, :], row_words[:, first_word + u : first_word + ROW_W : 2], identity[:]
                    )
            flipped_of[batch] = turned

        def copy_batch(batch):
            values = packed.tile([P, BATCH_GROUPS * P * PACK], BF16, align_bytes=64)
            nc.scalar.copy(
                out=values[:].bitcast(F32).rearrange("p (q c u) -> p q c u", q=BATCH_GROUPS, u=2),
                in_=flipped_of[batch][:].rearrange("p q u c -> p q c u"),
            )
            values_of[batch] = values

        def quantise_batch(batch):
            codes = quantised.tile([P, BATCH_GROUPS * P], I32, align_bytes=64)
            scales = quantised.tile([P, BATCH_GROUPS * P], U8, align_bytes=64)
            nc.vector.quantize_mx(out=codes[:].bitcast(FP8X4), scales=scales[:], in_=values_of[batch][:])
            codes_of[batch] = codes
            scales_of[batch] = scales

        def w_operands(variant, h):
            return dict(
                rhs=w_codes[:, (variant * HALVES + h) * 2 * BANK : (variant * HALVES + h + 1) * 2 * BANK].bitcast(FP4X4),
                rhs_scale=w_scales[:, (variant * HALVES + h) * BANK : (variant * HALVES + h + 1) * BANK],
            )

        def multiply(g):
            for s in range(PAIR):
                k = PAIR * g + s
                batch = k // BATCH
                group_columns = slice((k % BATCH) // GROUP * P, ((k % BATCH) // GROUP + 1) * P)
                node_columns = slice(((g % TURNS) * PAIR + s) * P, ((g % TURNS) * PAIR + s + 1) * P)
                for h in range(HALVES):
                    acc = sums.tile([P, BANK], F32)
                    if k % GROUP != WHOLE:
                        nc.tensor.matmul_mx(
                            out=acc[:],
                            lhsT=codes_of[batch][:, group_columns].bitcast(FP8X4),
                            lhsT_scale=scales_of[batch][:, group_columns],
                            start=True,
                            stop=False,
                            **w_operands(k % GROUP, h),
                        )
                    nc.tensor.matmul_mx(
                        out=acc[:],
                        lhsT=node_codes[:, node_columns].bitcast(FP8X4),
                        lhsT_scale=node_scales[:, node_columns],
                        start=k % GROUP == WHOLE,
                        stop=True,
                        **w_operands(WHOLE, h),
                    )
                    sums_of[(g, s, h)] = acc

        def leaky_relu(g, s):
            result = results.tile([P, HID], F32)
            for h in range(HALVES):
                acc = sums_of[(g, s, h)]
                part = result[:, h * BANK : (h + 1) * BANK]
                nc.scalar.copy(out=part, in_=acc[:])
                nc.vector.scalar_tensor_tensor(
                    out=part, in0=acc[:], scalar=NEG_SLOPE, in1=part, op0=ALU.mult, op1=ALU.max
                )
            k = PAIR * g + s
            nc.sync.dma_start(out=out_rows[:, k * HID : (k + 1) * HID], in_=result[:])

        transpose_batch(0)
        copy_batch(0)
        keep_src(0, PAIR)
        spread_codes(nc.gpsimd, 0)
        spread_scales(nc.vector, 0)
        quantise_batch(0)
        keep_src(PAIR, slots)
        spread_dst(1)
        for step in range(PAIRS + 1):
            ahead = step // BATCH_PAIRS + 1
            if ahead < BATCHES and step % BATCH_PAIRS == 0:
                transpose_batch(ahead)
            if step >= 1:
                leaky_relu(step - 1, 0)
            if ahead < BATCHES and step % BATCH_PAIRS == 2:
                quantise_batch(ahead)
            if ahead < BATCHES and step % BATCH_PAIRS == 1:
                copy_batch(ahead)
            if step + 2 < PAIRS:
                spread_dst(step + 2)
            if step >= 1:
                leaky_relu(step - 1, 1)
            if step < PAIRS:
                multiply(step)
